import numpy as np
import ml_dtypes


def mxq(x, axis, fmt="e4m3"):
    dtype, down = {"e4m3": (ml_dtypes.float8_e4m3fn, 7), "e5m2": (ml_dtypes.float8_e5m2, 14)}[fmt]
    v = np.moveaxis(np.asarray(x, np.float32).astype(ml_dtypes.bfloat16).astype(np.float64), axis, -1)
    blocks = v.reshape(v.shape[:-1] + (-1, 32))
    amax = np.abs(blocks).max(-1, keepdims=True)
    byte = np.maximum(np.where(amax > 0, np.frexp(amax)[1] - 1 + 127, 0) - down, 1)
    scale = np.exp2(byte - 127.0)
    codes = (blocks / scale).astype(np.float32).astype(dtype).astype(np.float64)
    return np.moveaxis((codes * scale).reshape(v.shape), -1, axis)


WIDE = False


def mx_kscale(k):
    if not WIDE:
        return np.ones(k)
    levels = np.array([10, -10, 5, -5, 0])
    a = np.random.permutation(np.resize(levels, k // 512 * 4)).reshape(k // 512, 4)
    idx = np.arange(k)
    return np.exp2(a[idx // 512, idx % 128 // 32])


BF16 = ml_dtypes.bfloat16


def bf(x):
    return np.asarray(x, np.float32).astype(BF16)


def f64(x):
    return np.asarray(x).astype(np.float64)


E2M1 = np.array([0.0, 0.5, 1.0, 1.5, 2.0, 3.0, 4.0, 6.0, -0.0, -0.5, -1.0, -1.5, -2.0, -3.0, -4.0, -6.0])


def pack_weight(w, fmt):
    k, n = w.shape
    w = f64(bf(w)).reshape(k // 32, 32, n)
    amax = np.abs(w).max(1)
    if fmt == "e4m3":
        byte = np.frexp(amax)[1] - 1 + 127 - 7
    else:
        mant, ex = np.frexp(amax / 6.0)
        byte = np.where(mant > 0.5, ex, ex - 1) + 127
    byte = np.clip(np.where(amax > 0, byte, 1), 1, 254)
    scaled = (w * np.exp2(127.0 - byte)[:, None, :]).reshape(k, n).astype(np.float32)
    by_word = np.ascontiguousarray(scaled.reshape(k // 512, 128, 4, n).transpose(0, 1, 3, 2))
    if fmt == "e4m3":
        words = by_word.astype(ml_dtypes.float8_e4m3fn).view(np.uint8)
    else:
        c = by_word.astype(ml_dtypes.float4_e2m1fn).view(np.uint8) & 0xF
        words = c[..., 0::2] | (c[..., 1::2] << 4)
    return np.ascontiguousarray(words), np.ascontiguousarray(byte.astype(np.uint8).reshape(k // 512, 16, n))


def unpack_weight(words, scales, fmt):
    g, p, n, _ = words.shape
    if fmt == "e4m3":
        vals = np.ascontiguousarray(words).view(ml_dtypes.float8_e4m3fn).astype(np.float64)
    else:
        nib = np.empty((g, p, n, 4), np.uint8)
        nib[..., 0::2] = words & 0xF
        nib[..., 1::2] = words >> 4
        vals = E2M1[nib]
    vals = vals * np.repeat(np.exp2(scales.astype(np.float64) - 127.0), 8, axis=1)[..., None]
    return vals.transpose(0, 1, 3, 2).reshape(g * 512, n)


B, N, H, T1 = 2, 4096, 512, 3072


def sigmoid(x):
    return 1.0 / (1.0 + np.exp(-x))


def setup_inputs():
    s = mx_kscale(H)
    w = 1.0 / np.sqrt(H)
    hidden_states = bf(np.random.standard_normal((B, N, H)))
    acc = bf(np.random.standard_normal((B, N, H)) * s)
    Wu_inter_words, Wu_inter_scales = pack_weight((np.random.standard_normal((H, H)) * w / s).T, "e4m3")
    bu_inter = bf(np.random.standard_normal(H) * 0.3)
    Wt_inter_words, Wt_inter_scales = pack_weight((np.random.standard_normal((H, H)) * w).T, "e4m3")
    bt_inter = bf(np.random.standard_normal(H) * 0.3)
    Wu_out_words, Wu_out_scales = pack_weight((np.random.standard_normal((H, H)) * w / s).T, "e4m3")
    bu_out = bf(np.random.standard_normal(H) * 0.3)
    Wt_out_words, Wt_out_scales = pack_weight((np.random.standard_normal((H, H)) * w).T, "e4m3")
    bt_out = bf(np.random.standard_normal(H) * 0.3)
    step_size = bf(0.5 + 0.5 * np.random.uniform(size=(1,)))
    return {"hidden_states": hidden_states,
            "acc": acc,
            "Wu_inter_words": Wu_inter_words,
            "Wu_inter_scales": Wu_inter_scales,
            "bu_inter": bu_inter,
            "Wt_inter_words": Wt_inter_words,
            "Wt_inter_scales": Wt_inter_scales,
            "bt_inter": bt_inter,
            "Wu_out_words": Wu_out_words,
            "Wu_out_scales": Wu_out_scales,
            "bu_out": bu_out,
            "Wt_out_words": Wt_out_words,
            "Wt_out_scales": Wt_out_scales,
            "bt_out": bt_out,
            "step_size": step_size}


def branch(h, hq, aq, Wu_words, Wu_scales, bu, Wt_words, Wt_scales, bt, step):
    dt = 2.0 * sigmoid((hq @ unpack_weight(Wt_words, Wt_scales, "e4m3")) + f64(bt)) - 1.0
    return h + step * dt * ((aq @ unpack_weight(Wu_words, Wu_scales, "e4m3")) + f64(bu))


def reference(hidden_states, acc, Wu_inter_words, Wu_inter_scales, bu_inter, Wt_inter_words, Wt_inter_scales, bt_inter, Wu_out_words, Wu_out_scales, bu_out, Wt_out_words, Wt_out_scales, bt_out, step_size):
    h = f64(hidden_states)
    hq = mxq(h, 2, "e4m3")
    aq = mxq(f64(acc), 2, "e4m3")
    step = f64(step_size)
    upd_inter = branch(h[:, :T1], hq[:, :T1], aq[:, :T1], Wu_inter_words, Wu_inter_scales, bu_inter, Wt_inter_words, Wt_inter_scales, bt_inter, step)
    upd_out = branch(h[:, T1:], hq[:, T1:], aq[:, T1:], Wu_out_words, Wu_out_scales, bu_out, Wt_out_words, Wt_out_scales, bt_out, step)
    return np.concatenate([upd_inter, upd_out], axis=1)

@@ -1,0 +1,272 @@
+from contextlib import ExitStack
+
+import concourse.mybir as mybir
+from concourse.masks import make_identity
+
+F32 = mybir.dt.float32
+BF16 = mybir.dt.bfloat16
+I32 = mybir.dt.int32
+U32 = mybir.dt.uint32
+U8 = mybir.dt.uint8
+FP8X4 = mybir.dt.float8_e4m3fn_x4
+ADD = mybir.AluOpType.add
+MULT = mybir.AluOpType.mult
+TANH = mybir.ActivationFunctionType.Tanh
+
+P = 128
+FEAT = 512
+PACK = 4
+SLICES = FEAT // P
+ROW_TILES = 4
+BLOCK_ROWS = ROW_TILES * P
+WORDS = FEAT // 2
+BATCH = 2
+NODES = 4096
+INTER_NODES = 3072
+BLOCKS = BATCH * NODES // BLOCK_ROWS
+BLOCKS_PER_BATCH = NODES // BLOCK_ROWS
+INTER_BLOCKS = INTER_NODES // BLOCK_ROWS
+STEPS = 2 * BLOCKS
+
+LOAD_AHEAD = 4
+TIN_AHEAD = 3
+TOUT_BEHIND = 3
+
+FLOPS = 2 * 2 * BATCH * NODES * FEAT * FEAT
+
+
+def tile_dynamicattentionnetwork_pb_t_kernel(
+    tc,
+    hidden_states,
+    acc,
+    Wu_inter_words,
+    Wu_inter_scales,
+    bu_inter,
+    Wt_inter_words,
+    Wt_inter_scales,
+    bt_inter,
+    Wu_out_words,
+    Wu_out_scales,
+    bu_out,
+    Wt_out_words,
+    Wt_out_scales,
+    bt_out,
+    step_size,
+    out,
+):
+    nc = tc.nc
+    x_blocks = [
+        x.flatten_outer_dims().rearrange("(c p r) k -> c p (r k)", p=P, r=ROW_TILES)
+        for x in (hidden_states, acc)
+    ]
+    out_blocks = out.flatten_outer_dims().rearrange("(c p r) n -> c p (r n)", p=P, r=ROW_TILES)
+    given = {
+        (0, "t"): (Wt_inter_words, Wt_inter_scales),
+        (0, "u"): (Wu_inter_words, Wu_inter_scales),
+        (1, "t"): (Wt_out_words, Wt_out_scales),
+        (1, "u"): (Wu_out_words, Wu_out_scales),
+    }
+    biases = (bt_inter, bt_out, bu_inter, bu_out)
+
+    with ExitStack() as ctx:
+        const = ctx.enter_context(tc.tile_pool(name="const", bufs=1))
+        h_pool = ctx.enter_context(tc.tile_pool(name="h_pool", bufs=6))
+        a_pool = ctx.enter_context(tc.tile_pool(name="a_pool", bufs=3))
+        grouped_pool = ctx.enter_context(tc.tile_pool(name="grouped_pool", bufs=3))
+        code_pool = ctx.enter_context(tc.tile_pool(name="code_pool", bufs=3))
+        gate_pool = ctx.enter_context(tc.tile_pool(name="gate_pool", bufs=3))
+        m_pool = ctx.enter_context(tc.tile_pool(name="m_pool", bufs=3))
+        o_pool = ctx.enter_context(tc.tile_pool(name="o_pool", bufs=3))
+        tin_pool = ctx.enter_context(tc.psum_pool(name="tin_pool", bufs=2))
+        mm_pool = ctx.enter_context(tc.psum_pool(name="mm_pool", bufs=2))
+        tout_pool = ctx.enter_context(tc.psum_pool(name="tout_pool", bufs=2))
+        ctx.enter_context(tc.manual_schedule())
+
+        x_tiles = {}
+        grouped_tiles = {}
+        code_tiles = {}
+        m_tiles = {}
+
+        def load(unit):
+            block, operand = divmod(unit, 2)
+            pool = a_pool if operand else h_pool
+            x_sb = pool.tile([P, ROW_TILES * FEAT], BF16, name="x_sb", tag="x_sb")
+            nc.sync.dma_start(out=x_sb[:], in_=x_blocks[operand][block])
+            x_tiles[unit] = x_sb
+
+        def load_words(key):
+            nc.sync.dma_start(
+                out=w_words[key][:].bitcast(I32),
+                in_=given[key][0].rearrange("g p n t -> (g p) (n t)").bitcast(I32),
+            )
+
+        def load_scales(key):
+            rows = given[key][1].rearrange("g (q r) n -> r (g q) n", r=4)
+            for r in range(4):
+                nc.sync.dma_start(
+                    out=w_planes[key][r:P:32, :].bitcast(I32), in_=rows[r].bitcast(I32)
+                )
+
+        def transpose_in(unit):
+            x_words = x_tiles[unit][:].bitcast(F32)
+            grouped = grouped_pool.tile(
+                [P, BLOCK_ROWS * PACK], BF16, name="grouped", tag="grouped", align_bytes=64
+            )
+            grouped_words = grouped[:].bitcast(F32).rearrange("p (c u) -> p c u", u=2)
+            for pair in range(ROW_TILES // 2):
+                bank = tin_pool.tile([P, 2, 2 * P], F32, name="tin", tag="tin")
+                for i in range(2):
+                    first = (2 * pair + i) * WORDS
+                    for u in range(2):
+                        nc.tensor.transpose(
+                            out=bank[:, u, i * P : (i + 1) * P],
+                            in_=x_words[:, first + u : first + WORDS : 2],
+                            identity=ident_f32[:],
+                        )
+                nc.scalar.copy(
+                    out=grouped_words[:, pair * 2 * P : (pair + 1) * 2 * P, :],
+                    in_=bank[:].rearrange("p u c -> p c u"),
+                )
+            grouped_tiles[unit] = grouped
+
+        def quantise(unit):
+            operand = unit % 2
+            codes = code_pool.tile(
+                [P, BLOCK_ROWS], U32, name="codes", tag="codes%d" % operand, align_bytes=64
+            )
+            plane = code_pool.tile(
+                [P, BLOCK_ROWS], U8, name="plane", tag="plane%d" % operand, align_bytes=64
+            )
+            nc.vector.quantize_mx(
+                out=codes[:].bitcast(FP8X4), scales=plane[:], in_=grouped_tiles[unit][:]
+            )
+            code_tiles[unit] = (codes, plane)
+
+        def multiply(step):
+            block, half = divmod(step, 2)
+            kind = 0 if block % BLOCKS_PER_BATCH < INTER_BLOCKS else 1
+            if half == 0:
+                m_tiles[block] = m_pool.tile([P, SLICES, BLOCK_ROWS], F32, name="m_sb", tag="m_sb")
+            for j in (2 * half, 2 * half + 1):
+                banks = {}
+                for branch, operand in (("t", 0), ("u", 1)):
+                    codes, plane = code_tiles[2 * block + operand]
+                    bank = mm_pool.tile([P, BLOCK_ROWS], F32, name="mm_" + branch, tag="mm_" + branch)
+                    nc.tensor.matmul_mx(
+                        out=bank[:],
+                        lhsT=w_words[(kind, branch)][:, j * P : (j + 1) * P].bitcast(FP8X4),
+                        lhsT_scale=w_planes[(kind, branch)][:, j * P : (j + 1) * P],
+                        rhs=codes[:].bitcast(FP8X4),
+                        rhs_scale=plane[:],
+                        start=True,
+                        stop=True,
+                    )
+                    banks[branch] = bank
+                column = SLICES * kind + j
+                gate = gate_pool.tile([P, BLOCK_ROWS], F32, name="gate", tag="gate")
+                nc.scalar.activation(
+                    out=gate[:],
+                    in_=banks["t"][:],
+                    func=TANH,
+                    bias=bt_half[:, column : column + 1],
+                    scale=0.5,
+                )
+                nc.vector.scalar_tensor_tensor(
+                    out=m_tiles[block][:, j, :],
+                    in0=banks["u"][:],
+                    scalar=bu_cols[:, column : column + 1],
+                    in1=gate[:],
+                    op0=ADD,
+                    op1=MULT,
+                )
+
+        def transpose_out(unit):
+            block, half = divmod(unit, 2)
+            o_sb = o_pool.tile([P, 2, FEAT], F32, name="o_sb", tag="o_sb")
+            for i in range(2):
+                r = 2 * half + i
+                bank = tout_pool.tile([P, FEAT], F32, name="tout", tag="tout")
+                for j in range(SLICES):
+                    nc.tensor.transpose(
+                        out=bank[:, j * P : (j + 1) * P],
+                        in_=m_tiles[block][:, j, r * P : (r + 1) * P],
+                        identity=ident_f32[:],
+                    )
+                nc.vector.scalar_tensor_tensor(
+                    out=o_sb[:, i, :],
+                    in0=bank[:],
+                    scalar=step_f32[:, 0:1],
+                    in1=x_tiles[2 * block][:, r * FEAT : (r + 1) * FEAT],
+                    op0=MULT,
+                    op1=ADD,
+                )
+            nc.sync.dma_start(
+                out=out_blocks[block][:, half * 2 * FEAT : (half + 1) * 2 * FEAT],
+                in_=o_sb[:].rearrange("p i n -> p (i n)"),
+            )
+
+        w_words = {}
+        w_planes = {}
+        for key in given:
+            w_words[key] = const.tile(
+                [P, FEAT], U32, name="w_words", tag="w_words%d%s" % key, align_bytes=64
+            )
+            w_planes[key] = const.tile(
+                [P, FEAT], U8, name="w_plane", tag="w_plane%d%s" % key, align_bytes=64
+            )
+            nc.vector.memset(w_planes[key][:].bitcast(I32), 0)
+        bias_rows = const.tile([P, P], BF16, name="bias_rows")
+        nc.vector.memset(bias_rows[:], 0.0)
+        zero = const.tile([P, 1], F32, name="zero")
+        nc.vector.memset(zero[:], 0.0)
+        table_warm = const.tile([P, 1], F32, name="table_warm")
+        nc.scalar.activation(out=table_warm[:], in_=zero[:], func=TANH)
+
+        ident_f32 = const.tile([P, P], F32, name="ident_f32")
+        make_identity(nc, ident_f32[:])
+        ident_bf16 = const.tile([P, P], BF16, name="ident_bf16")
+        nc.vector.tensor_copy(out=ident_bf16[:], in_=ident_f32[:])
+
+        for i, bias in enumerate(biases):
+            nc.gpsimd.dma_start(
+                out=bias_rows[SLICES * i : SLICES * (i + 1), :],
+                in_=bias.rearrange("(j p) -> j p", p=P),
+            )
+        step_bf16 = const.tile([P, 1], BF16, name="step_bf16")
+        nc.gpsimd.dma_start(out=step_bf16[:], in_=step_size.partition_broadcast(P))
+        bt_half = const.tile([P, 2 * SLICES], F32, name="bt_half")
+        bu_cols = const.tile([P, 2 * SLICES], F32, name="bu_cols")
+        step_f32 = const.tile([P, 1], F32, name="step_f32")
+
+        def spread_biases():
+            bias_ps = tin_pool.tile([P, P], BF16, name="bias_ps", tag="tin")
+            nc.tensor.transpose(out=bias_ps[:], in_=bias_rows[:], identity=ident_bf16[:])
+            nc.vector.tensor_scalar_mul(out=bt_half[:], in0=bias_ps[:, 0 : 2 * SLICES], scalar1=0.5)
+            nc.vector.tensor_copy(out=bu_cols[:], in_=bias_ps[:, 2 * SLICES : 4 * SLICES])
+            nc.vector.tensor_copy(out=step_f32[:], in_=step_bf16[:])
+
+        load(0)
+        load(1)
+        load_scales((0, "t"))
+        load(2)
+        load(3)
+        load_words((0, "t"))
+        load_words((0, "u"))
+        load_scales((0, "u"))
+
+        for step in range(-TIN_AHEAD, STEPS + TOUT_BEHIND):
+            if step + TIN_AHEAD + LOAD_AHEAD < STEPS:
+                load(step + TIN_AHEAD + LOAD_AHEAD)
+            if step == 0:
+                spread_biases()
+                for branch in ("t", "u"):
+                    load_words((1, branch))
+                    load_scales((1, branch))
+            if step - TOUT_BEHIND >= 0:
+                transpose_out(step - TOUT_BEHIND)
+            if step + TIN_AHEAD < STEPS:
+                transpose_in(step + TIN_AHEAD)
+            if 0 <= step + TIN_AHEAD - 1 < STEPS:
+                quantise(step + TIN_AHEAD - 1)
+            if 0 <= step < STEPS:
+                multiply(step)

@@ -76,7 +76,7 @@ def tile_dynamicattentionnetwork_pb_t_kernel(
         code_pool = ctx.enter_context(tc.tile_pool(name="code_pool", bufs=3))
         gate_pool = ctx.enter_context(tc.tile_pool(name="gate_pool", bufs=3))
         m_pool = ctx.enter_context(tc.tile_pool(name="m_pool", bufs=3))
-        o_pool = ctx.enter_context(tc.tile_pool(name="o_pool", bufs=3))
+        o_pool = ctx.enter_context(tc.tile_pool(name="o_pool", bufs=6))
         tin_pool = ctx.enter_context(tc.psum_pool(name="tin_pool", bufs=2))
         mm_pool = ctx.enter_context(tc.psum_pool(name="mm_pool", bufs=2))
         tout_pool = ctx.enter_context(tc.psum_pool(name="tout_pool", bufs=2))
@@ -182,9 +182,8 @@ def tile_dynamicattentionnetwork_pb_t_kernel(
 
         def transpose_out(unit):
             block, half = divmod(unit, 2)
-            o_sb = o_pool.tile([P, 2, FEAT], F32, name="o_sb", tag="o_sb")
-            for i in range(2):
-                r = 2 * half + i
+            for r in (2 * half, 2 * half + 1):
+                o_sb = o_pool.tile([P, FEAT], F32, name="o_sb", tag="o_sb")
                 bank = tout_pool.tile([P, FEAT], F32, name="tout", tag="tout")
                 for j in range(SLICES):
                     nc.tensor.transpose(
@@ -193,17 +192,14 @@ def tile_dynamicattentionnetwork_pb_t_kernel(
                         identity=ident_f32[:],
                     )
                 nc.vector.scalar_tensor_tensor(
-                    out=o_sb[:, i, :],
+                    out=o_sb[:],
                     in0=bank[:],
                     scalar=step_f32[:, 0:1],
                     in1=x_tiles[2 * block][:, r * FEAT : (r + 1) * FEAT],
                     op0=MULT,
                     op1=ADD,
                 )
-            nc.sync.dma_start(
-                out=out_blocks[block][:, half * 2 * FEAT : (half + 1) * 2 * FEAT],
-                in_=o_sb[:].rearrange("p i n -> p (i n)"),
-            )
+                nc.sync.dma_start(out=out_blocks[block][:, r * FEAT : (r + 1) * FEAT], in_=o_sb[:])
 
         w_words = {}
         w_planes = {}
@@ -264,9 +260,9 @@ def tile_dynamicattentionnetwork_pb_t_kernel(
                     load_scales((1, branch))
             if step - TOUT_BEHIND >= 0:
                 transpose_out(step - TOUT_BEHIND)
-            if step + TIN_AHEAD < STEPS:
-                transpose_in(step + TIN_AHEAD)
             if 0 <= step + TIN_AHEAD - 1 < STEPS:
                 quantise(step + TIN_AHEAD - 1)
             if 0 <= step < STEPS:
                 multiply(step)
+            if step + TIN_AHEAD < STEPS:
+                transpose_in(step + TIN_AHEAD)

@@ -17,20 +17,19 @@ P = 128
 FEAT = 512
 PACK = 4
 SLICES = FEAT // P
-ROW_TILES = 4
-BLOCK_ROWS = ROW_TILES * P
+ROW_TILES = 2
+ROWS = ROW_TILES * P
 WORDS = FEAT // 2
 BATCH = 2
 NODES = 4096
 INTER_NODES = 3072
-BLOCKS = BATCH * NODES // BLOCK_ROWS
-BLOCKS_PER_BATCH = NODES // BLOCK_ROWS
-INTER_BLOCKS = INTER_NODES // BLOCK_ROWS
-STEPS = 2 * BLOCKS
+GROUPS = BATCH * NODES // ROWS
+GROUPS_PER_BATCH = NODES // ROWS
+INTER_GROUPS = INTER_NODES // ROWS
 
-LOAD_AHEAD = 4
-TIN_AHEAD = 3
-TOUT_BEHIND = 3
+LOAD_AHEAD = 3
+TIN_AHEAD = 2
+TOUT_BEHIND = 2
 
 FLOPS = 2 * 2 * BATCH * NODES * FEAT * FEAT
 
@@ -55,11 +54,9 @@ def tile_dynamicattentionnetwork_pb_t_kernel(
     out,
 ):
     nc = tc.nc
-    x_blocks = [
-        x.flatten_outer_dims().rearrange("(c p r) k -> c p (r k)", p=P, r=ROW_TILES)
-        for x in (hidden_states, acc)
-    ]
-    out_blocks = out.flatten_outer_dims().rearrange("(c p r) n -> c p (r n)", p=P, r=ROW_TILES)
+    h_groups = hidden_states.flatten_outer_dims().rearrange("(c p r) k -> c p (r k)", p=P, r=ROW_TILES)
+    a_groups = acc.flatten_outer_dims().rearrange("(c p r) k -> c p (r k)", p=P, r=ROW_TILES)
+    out_groups = out.flatten_outer_dims().rearrange("(c p r) n -> c p (r n)", p=P, r=ROW_TILES)
     given = {
         (0, "t"): (Wt_inter_words, Wt_inter_scales),
         (0, "u"): (Wu_inter_words, Wu_inter_scales),
@@ -70,15 +67,15 @@ def tile_dynamicattentionnetwork_pb_t_kernel(
 
     with ExitStack() as ctx:
         const = ctx.enter_context(tc.tile_pool(name="const", bufs=1))
-        h_pool = ctx.enter_context(tc.tile_pool(name="h_pool", bufs=6))
-        a_pool = ctx.enter_context(tc.tile_pool(name="a_pool", bufs=3))
+        h_pool = ctx.enter_context(tc.tile_pool(name="h_pool", bufs=LOAD_AHEAD + TIN_AHEAD + TOUT_BEHIND + 1))
+        a_pool = ctx.enter_context(tc.tile_pool(name="a_pool", bufs=LOAD_AHEAD + 1))
         grouped_pool = ctx.enter_context(tc.tile_pool(name="grouped_pool", bufs=3))
         code_pool = ctx.enter_context(tc.tile_pool(name="code_pool", bufs=3))
-        gate_pool = ctx.enter_context(tc.tile_pool(name="gate_pool", bufs=3))
-        m_pool = ctx.enter_context(tc.tile_pool(name="m_pool", bufs=3))
+        gate_pool = ctx.enter_context(tc.tile_pool(name="gate_pool", bufs=SLICES))
+        m_pool = ctx.enter_context(tc.tile_pool(name="m_pool", bufs=TOUT_BEHIND + 1))
         o_pool = ctx.enter_context(tc.tile_pool(name="o_pool", bufs=6))
         tin_pool = ctx.enter_context(tc.psum_pool(name="tin_pool", bufs=2))
-        mm_pool = ctx.enter_context(tc.psum_pool(name="mm_pool", bufs=2))
+        mm_pool = ctx.enter_context(tc.psum_pool(name="mm_pool", bufs=SLICES))
         tout_pool = ctx.enter_context(tc.psum_pool(name="tout_pool", bufs=2))
         ctx.enter_context(tc.manual_schedule())
 
@@ -87,12 +84,12 @@ def tile_dynamicattentionnetwork_pb_t_kernel(
         code_tiles = {}
         m_tiles = {}
 
-        def load(unit):
-            block, operand = divmod(unit, 2)
-            pool = a_pool if operand else h_pool
-            x_sb = pool.tile([P, ROW_TILES * FEAT], BF16, name="x_sb", tag="x_sb")
-            nc.sync.dma_start(out=x_sb[:], in_=x_blocks[operand][block])
-            x_tiles[unit] = x_sb
+        def load(group):
+            h_sb = h_pool.tile([P, ROW_TILES * FEAT], BF16, name="h_sb", tag="h_sb")
+            nc.sync.dma_start(out=h_sb[:], in_=h_groups[group])
+            a_sb = a_pool.tile([P, ROW_TILES * FEAT], BF16, name="a_sb", tag="a_sb")
+            nc.sync.dma_start(out=a_sb[:], in_=a_groups[group])
+            x_tiles[group] = (h_sb, a_sb)
 
         def load_words(key):
             nc.sync.dma_start(
@@ -107,99 +104,90 @@ def tile_dynamicattentionnetwork_pb_t_kernel(
                     out=w_planes[key][r:P:32, :].bitcast(I32), in_=rows[r].bitcast(I32)
                 )
 
-        def transpose_in(unit):
-            x_words = x_tiles[unit][:].bitcast(F32)
+        def transpose_in(group):
             grouped = grouped_pool.tile(
-                [P, BLOCK_ROWS * PACK], BF16, name="grouped", tag="grouped", align_bytes=64
+                [P, 2, ROWS * PACK], BF16, name="grouped", tag="grouped", align_bytes=64
             )
-            grouped_words = grouped[:].bitcast(F32).rearrange("p (c u) -> p c u", u=2)
-            for pair in range(ROW_TILES // 2):
-                bank = tin_pool.tile([P, 2, 2 * P], F32, name="tin", tag="tin")
-                for i in range(2):
-                    first = (2 * pair + i) * WORDS
+            for operand in range(2):
+                x_words = x_tiles[group][operand][:].bitcast(F32)
+                bank = tin_pool.tile([P, 2, ROWS], F32, name="tin", tag="tin")
+                for i in range(ROW_TILES):
                     for u in range(2):
                         nc.tensor.transpose(
                             out=bank[:, u, i * P : (i + 1) * P],
-                            in_=x_words[:, first + u : first + WORDS : 2],
+                            in_=x_words[:, i * WORDS + u : (i + 1) * WORDS : 2],
                             identity=ident_f32[:],
                         )
                 nc.scalar.copy(
-                    out=grouped_words[:, pair * 2 * P : (pair + 1) * 2 * P, :],
+                    out=grouped[:, operand, :].bitcast(F32).rearrange("p (c u) -> p c u", u=2),
                     in_=bank[:].rearrange("p u c -> p c u"),
                 )
-            grouped_tiles[unit] = grouped
+            grouped_tiles[group] = grouped
 
-        def quantise(unit):
-            operand = unit % 2
-            codes = code_pool.tile(
-                [P, BLOCK_ROWS], U32, name="codes", tag="codes%d" % operand, align_bytes=64
-            )
-            plane = code_pool.tile(
-                [P, BLOCK_ROWS], U8, name="plane", tag="plane%d" % operand, align_bytes=64
-            )
+        def quantise(group):
+            codes = code_pool.tile([P, 2, ROWS], U32, name="codes", tag="codes", align_bytes=64)
+            plane = code_pool.tile([P, 2, ROWS], U8, name="plane", tag="plane", align_bytes=64)
             nc.vector.quantize_mx(
-                out=codes[:].bitcast(FP8X4), scales=plane[:], in_=grouped_tiles[unit][:]
+                out=codes[:].rearrange("p o c -> p (o c)").bitcast(FP8X4),
+                scales=plane[:].rearrange("p o c -> p (o c)"),
+                in_=grouped_tiles[group][:].rearrange("p o c -> p (o c)"),
             )
-            code_tiles[unit] = (codes, plane)
+            code_tiles[group] = (codes, plane)
 
-        def multiply(step):
-            block, half = divmod(step, 2)
-            kind = 0 if block % BLOCKS_PER_BATCH < INTER_BLOCKS else 1
-            if half == 0:
-                m_tiles[block] = m_pool.tile([P, SLICES, BLOCK_ROWS], F32, name="m_sb", tag="m_sb")
-            for j in (2 * half, 2 * half + 1):
-                banks = {}
-                for branch, operand in (("t", 0), ("u", 1)):
-                    codes, plane = code_tiles[2 * block + operand]
-                    bank = mm_pool.tile([P, BLOCK_ROWS], F32, name="mm_" + branch, tag="mm_" + branch)
+        def multiply(group):
+            kind = 0 if group % GROUPS_PER_BATCH < INTER_GROUPS else 1
+            codes, plane = code_tiles[group]
+            m_sb = m_pool.tile([P, SLICES, ROWS], F32, name="m_sb", tag="m_sb")
+            for j in range(SLICES):
+                bank = mm_pool.tile([P, 2, ROWS], F32, name="mm", tag="mm")
+                for branch, operand in (("u", 1), ("t", 0)):
                     nc.tensor.matmul_mx(
-                        out=bank[:],
+                        out=bank[:, operand, :],
                         lhsT=w_words[(kind, branch)][:, j * P : (j + 1) * P].bitcast(FP8X4),
                         lhsT_scale=w_planes[(kind, branch)][:, j * P : (j + 1) * P],
-                        rhs=codes[:].bitcast(FP8X4),
-                        rhs_scale=plane[:],
+                        rhs=codes[:, operand, :].bitcast(FP8X4),
+                        rhs_scale=plane[:, operand, :],
                         start=True,
                         stop=True,
                     )
-                    banks[branch] = bank
                 column = SLICES * kind + j
-                gate = gate_pool.tile([P, BLOCK_ROWS], F32, name="gate", tag="gate")
+                gate = gate_pool.tile([P, ROWS], F32, name="gate", tag="gate")
                 nc.scalar.activation(
                     out=gate[:],
-                    in_=banks["t"][:],
+                    in_=bank[:, 0, :],
                     func=TANH,
                     bias=bt_half[:, column : column + 1],
                     scale=0.5,
                 )
                 nc.vector.scalar_tensor_tensor(
-                    out=m_tiles[block][:, j, :],
-                    in0=banks["u"][:],
+                    out=m_sb[:, j, :],
+                    in0=bank[:, 1, :],
                     scalar=bu_cols[:, column : column + 1],
                     in1=gate[:],
                     op0=ADD,
                     op1=MULT,
                 )
+            m_tiles[group] = m_sb
 
-        def transpose_out(unit):
-            block, half = divmod(unit, 2)
-            for r in (2 * half, 2 * half + 1):
-                o_sb = o_pool.tile([P, FEAT], F32, name="o_sb", tag="o_sb")
+        def transpose_out(group):
+            for i in range(ROW_TILES):
                 bank = tout_pool.tile([P, FEAT], F32, name="tout", tag="tout")
                 for j in range(SLICES):
                     nc.tensor.transpose(
                         out=bank[:, j * P : (j + 1) * P],
-                        in_=m_tiles[block][:, j, r * P : (r + 1) * P],
+                        in_=m_tiles[group][:, j, i * P : (i + 1) * P],
                         identity=ident_f32[:],
                     )
+                o_sb = o_pool.tile([P, FEAT], F32, name="o_sb", tag="o_sb")
                 nc.vector.scalar_tensor_tensor(
                     out=o_sb[:],
                     in0=bank[:],
                     scalar=step_f32[:, 0:1],
-                    in1=x_tiles[2 * block][:, r * FEAT : (r + 1) * FEAT],
+                    in1=x_tiles[group][0][:, i * FEAT : (i + 1) * FEAT],
                     op0=MULT,
                     op1=ADD,
                 )
-                nc.sync.dma_start(out=out_blocks[block][:, r * FEAT : (r + 1) * FEAT], in_=o_sb[:])
+                nc.sync.dma_start(out=out_groups[group][:, i * FEAT : (i + 1) * FEAT], in_=o_sb[:])
 
         w_words = {}
         w_planes = {}
@@ -242,27 +230,26 @@ def tile_dynamicattentionnetwork_pb_t_kernel(
             nc.vector.tensor_copy(out=step_f32[:], in_=step_bf16[:])
 
         load(0)
+        load_scales((0, "u"))
         load(1)
+        load_words((0, "u"))
+        load_words((0, "t"))
         load_scales((0, "t"))
         load(2)
-        load(3)
-        load_words((0, "t"))
-        load_words((0, "u"))
-        load_scales((0, "u"))
 
-        for step in range(-TIN_AHEAD, STEPS + TOUT_BEHIND):
-            if step + TIN_AHEAD + LOAD_AHEAD < STEPS:
+        for step in range(-TIN_AHEAD, GROUPS + TOUT_BEHIND):
+            if step + TIN_AHEAD + LOAD_AHEAD < GROUPS:
                 load(step + TIN_AHEAD + LOAD_AHEAD)
             if step == 0:
                 spread_biases()
-                for branch in ("t", "u"):
+                for branch in ("u", "t"):
                     load_words((1, branch))
                     load_scales((1, branch))
             if step - TOUT_BEHIND >= 0:
                 transpose_out(step - TOUT_BEHIND)
-            if 0 <= step + TIN_AHEAD - 1 < STEPS:
+            if 0 <= step + TIN_AHEAD - 1 < GROUPS:
                 quantise(step + TIN_AHEAD - 1)
-            if 0 <= step < STEPS:
+            if 0 <= step < GROUPS:
                 multiply(step)
-            if step + TIN_AHEAD < STEPS:
+            if step + TIN_AHEAD < GROUPS:
                 transpose_in(step + TIN_AHEAD)

@@ -77,7 +77,6 @@ def tile_dynamicattentionnetwork_pb_t_kernel(
         tin_pool = ctx.enter_context(tc.psum_pool(name="tin_pool", bufs=2))
         mm_pool = ctx.enter_context(tc.psum_pool(name="mm_pool", bufs=SLICES))
         tout_pool = ctx.enter_context(tc.psum_pool(name="tout_pool", bufs=2))
-        ctx.enter_context(tc.manual_schedule())
 
         x_tiles = {}
         grouped_tiles = {}

@@ -70,6 +70,7 @@ def tile_dynamicattentionnetwork_pb_t_kernel(
         h_pool = ctx.enter_context(tc.tile_pool(name="h_pool", bufs=LOAD_AHEAD + TIN_AHEAD + TOUT_BEHIND + 1))
         a_pool = ctx.enter_context(tc.tile_pool(name="a_pool", bufs=LOAD_AHEAD + 1))
         grouped_pool = ctx.enter_context(tc.tile_pool(name="grouped_pool", bufs=3))
+        split_pool = ctx.enter_context(tc.tile_pool(name="split_pool", bufs=3))
         code_pool = ctx.enter_context(tc.tile_pool(name="code_pool", bufs=3))
         gate_pool = ctx.enter_context(tc.tile_pool(name="gate_pool", bufs=SLICES))
         m_pool = ctx.enter_context(tc.tile_pool(name="m_pool", bufs=TOUT_BEHIND + 1))
@@ -79,6 +80,7 @@ def tile_dynamicattentionnetwork_pb_t_kernel(
         tout_pool = ctx.enter_context(tc.psum_pool(name="tout_pool", bufs=2))
 
         x_tiles = {}
+        split_tiles = {}
         grouped_tiles = {}
         code_tiles = {}
         m_tiles = {}
@@ -103,18 +105,30 @@ def tile_dynamicattentionnetwork_pb_t_kernel(
                     out=w_planes[key][r:P:32, :].bitcast(I32), in_=rows[r].bitcast(I32)
                 )
 
+        def split(group):
+            a_split = split_pool.tile([P, ROW_TILES, 2, P], F32, name="a_split", tag="a_split")
+            nc.scalar.copy(
+                out=a_split[:],
+                in_=x_tiles[group][1][:].bitcast(F32).rearrange("p (i w u) -> p i u w", i=ROW_TILES, u=2),
+            )
+            split_tiles[group] = a_split
+
         def transpose_in(group):
             grouped = grouped_pool.tile(
                 [P, 2, ROWS * PACK], BF16, name="grouped", tag="grouped", align_bytes=64
             )
             for operand in range(2):
-                x_words = x_tiles[group][operand][:].bitcast(F32)
+                h_words = x_tiles[group][0][:].bitcast(F32)
                 bank = tin_pool.tile([P, 2, ROWS], F32, name="tin", tag="tin")
                 for i in range(ROW_TILES):
                     for u in range(2):
                         nc.tensor.transpose(
                             out=bank[:, u, i * P : (i + 1) * P],
-                            in_=x_words[:, i * WORDS + u : (i + 1) * WORDS : 2],
+                            in_=(
+                                split_tiles[group][:, i, u, :]
+                                if operand == 1
+                                else h_words[:, i * WORDS + u : (i + 1) * WORDS : 2]
+                            ),
                             identity=ident_f32[:],
                         )
                 nc.scalar.copy(
@@ -250,5 +264,9 @@ def tile_dynamicattentionnetwork_pb_t_kernel(
                 quantise(step + TIN_AHEAD - 1)
             if 0 <= step < GROUPS:
                 multiply(step)
+            if step == -TIN_AHEAD:
+                split(0)
             if step + TIN_AHEAD < GROUPS:
                 transpose_in(step + TIN_AHEAD)
+            if step + TIN_AHEAD + 1 < GROUPS:
+                split(step + TIN_AHEAD + 1)

@@ -29,6 +29,7 @@ INTER_GROUPS = INTER_NODES // ROWS
 
 LOAD_AHEAD = 3
 TIN_AHEAD = 2
+FIRST_SPLIT = 2
 TOUT_BEHIND = 2
 
 FLOPS = 2 * 2 * BATCH * NODES * FEAT * FEAT
@@ -63,7 +64,7 @@ def tile_dynamicattentionnetwork_pb_t_kernel(
         (1, "t"): (Wt_out_words, Wt_out_scales),
         (1, "u"): (Wu_out_words, Wu_out_scales),
     }
-    biases = (bt_inter, bt_out, bu_inter, bu_out)
+    biases = ((bt_inter, bu_inter), (bt_out, bu_out))
 
     with ExitStack() as ctx:
         const = ctx.enter_context(tc.tile_pool(name="const", bufs=1))
@@ -74,7 +75,7 @@ def tile_dynamicattentionnetwork_pb_t_kernel(
         code_pool = ctx.enter_context(tc.tile_pool(name="code_pool", bufs=3))
         gate_pool = ctx.enter_context(tc.tile_pool(name="gate_pool", bufs=SLICES))
         m_pool = ctx.enter_context(tc.tile_pool(name="m_pool", bufs=TOUT_BEHIND + 1))
-        o_pool = ctx.enter_context(tc.tile_pool(name="o_pool", bufs=6))
+        o_pool = ctx.enter_context(tc.tile_pool(name="o_pool", bufs=GROUPS * ROW_TILES))
         tin_pool = ctx.enter_context(tc.psum_pool(name="tin_pool", bufs=2))
         mm_pool = ctx.enter_context(tc.psum_pool(name="mm_pool", bufs=SLICES))
         tout_pool = ctx.enter_context(tc.psum_pool(name="tout_pool", bufs=2))
@@ -118,7 +119,7 @@ def tile_dynamicattentionnetwork_pb_t_kernel(
                 [P, 2, ROWS * PACK], BF16, name="grouped", tag="grouped", align_bytes=64
             )
             for operand in range(2):
-                h_words = x_tiles[group][0][:].bitcast(F32)
+                x_words = x_tiles[group][operand][:].bitcast(F32)
                 bank = tin_pool.tile([P, 2, ROWS], F32, name="tin", tag="tin")
                 for i in range(ROW_TILES):
                     for u in range(2):
@@ -126,8 +127,8 @@ def tile_dynamicattentionnetwork_pb_t_kernel(
                             out=bank[:, u, i * P : (i + 1) * P],
                             in_=(
                                 split_tiles[group][:, i, u, :]
-                                if operand == 1
-                                else h_words[:, i * WORDS + u : (i + 1) * WORDS : 2]
+                                if operand == 1 and group >= FIRST_SPLIT
+                                else x_words[:, i * WORDS + u : (i + 1) * WORDS : 2]
                             ),
                             identity=ident_f32[:],
                         )
@@ -202,6 +203,10 @@ def tile_dynamicattentionnetwork_pb_t_kernel(
                 )
                 nc.sync.dma_start(out=out_groups[group][:, i * FEAT : (i + 1) * FEAT], in_=o_sb[:])
 
+        bias_rows = {}
+        for kind in range(2):
+            bias_rows[kind] = const.tile([P, P], BF16, name="bias_rows", tag="bias_rows%d" % kind)
+            nc.vector.memset(bias_rows[kind][:], 0.0)
         w_words = {}
         w_planes = {}
         for key in given:
@@ -212,8 +217,6 @@ def tile_dynamicattentionnetwork_pb_t_kernel(
                 [P, FEAT], U8, name="w_plane", tag="w_plane%d%s" % key, align_bytes=64
             )
             nc.vector.memset(w_planes[key][:].bitcast(I32), 0)
-        bias_rows = const.tile([P, P], BF16, name="bias_rows")
-        nc.vector.memset(bias_rows[:], 0.0)
         zero = const.tile([P, 1], F32, name="zero")
         nc.vector.memset(zero[:], 0.0)
         table_warm = const.tile([P, 1], F32, name="table_warm")
@@ -224,23 +227,25 @@ def tile_dynamicattentionnetwork_pb_t_kernel(
         ident_bf16 = const.tile([P, P], BF16, name="ident_bf16")
         nc.vector.tensor_copy(out=ident_bf16[:], in_=ident_f32[:])
 
-        for i, bias in enumerate(biases):
-            nc.gpsimd.dma_start(
-                out=bias_rows[SLICES * i : SLICES * (i + 1), :],
-                in_=bias.rearrange("(j p) -> j p", p=P),
-            )
+        def load_biases(kind):
+            for i, bias in enumerate(biases[kind]):
+                nc.gpsimd.dma_start(
+                    out=bias_rows[kind][SLICES * i : SLICES * (i + 1), :],
+                    in_=bias.rearrange("(j p) -> j p", p=P),
+                )
+
+        load_biases(0)
         step_bf16 = const.tile([P, 1], BF16, name="step_bf16")
-        nc.gpsimd.dma_start(out=step_bf16[:], in_=step_size.partition_broadcast(P))
         bt_half = const.tile([P, 2 * SLICES], F32, name="bt_half")
         bu_cols = const.tile([P, 2 * SLICES], F32, name="bu_cols")
         step_f32 = const.tile([P, 1], F32, name="step_f32")
 
-        def spread_biases():
+        def spread_biases(kind):
             bias_ps = tin_pool.tile([P, P], BF16, name="bias_ps", tag="tin")
-            nc.tensor.transpose(out=bias_ps[:], in_=bias_rows[:], identity=ident_bf16[:])
-            nc.vector.tensor_scalar_mul(out=bt_half[:], in0=bias_ps[:, 0 : 2 * SLICES], scalar1=0.5)
-            nc.vector.tensor_copy(out=bu_cols[:], in_=bias_ps[:, 2 * SLICES : 4 * SLICES])
-            nc.vector.tensor_copy(out=step_f32[:], in_=step_bf16[:])
+            nc.tensor.transpose(out=bias_ps[:], in_=bias_rows[kind][:], identity=ident_bf16[:])
+            cols = slice(SLICES * kind, SLICES * (kind + 1))
+            nc.vector.tensor_scalar_mul(out=bt_half[:, cols], in0=bias_ps[:, 0:SLICES], scalar1=0.5)
+            nc.vector.tensor_copy(out=bu_cols[:, cols], in_=bias_ps[:, SLICES : 2 * SLICES])
 
         load(0)
         load_scales((0, "u"))
@@ -254,19 +259,22 @@ def tile_dynamicattentionnetwork_pb_t_kernel(
             if step + TIN_AHEAD + LOAD_AHEAD < GROUPS:
                 load(step + TIN_AHEAD + LOAD_AHEAD)
             if step == 0:
-                spread_biases()
+                nc.gpsimd.dma_start(out=step_bf16[:], in_=step_size.partition_broadcast(P))
+                load_biases(1)
+                spread_biases(0)
                 for branch in ("u", "t"):
                     load_words((1, branch))
                     load_scales((1, branch))
+            if step == 1:
+                nc.vector.tensor_copy(out=step_f32[:], in_=step_bf16[:])
+                spread_biases(1)
             if step - TOUT_BEHIND >= 0:
                 transpose_out(step - TOUT_BEHIND)
             if 0 <= step + TIN_AHEAD - 1 < GROUPS:
                 quantise(step + TIN_AHEAD - 1)
             if 0 <= step < GROUPS:
                 multiply(step)
-            if step == -TIN_AHEAD:
-                split(0)
             if step + TIN_AHEAD < GROUPS:
                 transpose_in(step + TIN_AHEAD)
-            if step + TIN_AHEAD + 1 < GROUPS:
+            if FIRST_SPLIT <= step + TIN_AHEAD + 1 < GROUPS:
                 split(step + TIN_AHEAD + 1)

@@ -29,7 +29,7 @@ INTER_GROUPS = INTER_NODES // ROWS
 
 LOAD_AHEAD = 3
 TIN_AHEAD = 2
-FIRST_SPLIT = 2
+FIRST_SPLIT = 5
 TOUT_BEHIND = 2
 
 FLOPS = 2 * 2 * BATCH * NODES * FEAT * FEAT
@@ -193,15 +193,21 @@ def tile_dynamicattentionnetwork_pb_t_kernel(
                         identity=ident_f32[:],
                     )
                 o_sb = o_pool.tile([P, FEAT], F32, name="o_sb", tag="o_sb")
-                nc.vector.scalar_tensor_tensor(
-                    out=o_sb[:],
-                    in0=bank[:],
-                    scalar=step_f32[:, 0:1],
-                    in1=x_tiles[group][0][:, i * FEAT : (i + 1) * FEAT],
-                    op0=MULT,
-                    op1=ADD,
-                )
-                nc.sync.dma_start(out=out_groups[group][:, i * FEAT : (i + 1) * FEAT], in_=o_sb[:])
+                pieces = 2 if group == GROUPS - 1 and i == ROW_TILES - 1 else 1
+                for piece in range(pieces):
+                    cols = slice(piece * FEAT // pieces, (piece + 1) * FEAT // pieces)
+                    row_cols = slice(i * FEAT + cols.start, i * FEAT + cols.stop)
+                    nc.vector.scalar_tensor_tensor(
+                        out=o_sb[:, cols],
+                        in0=bank[:, cols],
+                        scalar=step_f32[:, 0:1],
+                        in1=x_tiles[group][0][:, row_cols],
+                        op0=MULT,
+                        op1=ADD,
+                    )
+                    nc.sync.dma_start(out=out_groups[group][:, row_cols], in_=o_sb[:, cols])
+
+        ctx.enter_context(tc.manual_schedule(engines={mybir.EngineType.Pool}))
 
         bias_rows = {}
         for kind in range(2):
@@ -236,12 +242,14 @@ def tile_dynamicattentionnetwork_pb_t_kernel(
 
         load_biases(0)
         step_bf16 = const.tile([P, 1], BF16, name="step_bf16")
+        nc.gpsimd.dma_start(out=step_bf16[:], in_=step_size.partition_broadcast(P))
+        load_biases(1)
         bt_half = const.tile([P, 2 * SLICES], F32, name="bt_half")
         bu_cols = const.tile([P, 2 * SLICES], F32, name="bu_cols")
         step_f32 = const.tile([P, 1], F32, name="step_f32")
 
         def spread_biases(kind):
-            bias_ps = tin_pool.tile([P, P], BF16, name="bias_ps", tag="tin")
+            bias_ps = tout_pool.tile([P, P], BF16, name="bias_ps", tag="tout")
             nc.tensor.transpose(out=bias_ps[:], in_=bias_rows[kind][:], identity=ident_bf16[:])
             cols = slice(SLICES * kind, SLICES * (kind + 1))
             nc.vector.tensor_scalar_mul(out=bt_half[:, cols], in0=bias_ps[:, 0:SLICES], scalar1=0.5)
@@ -259,14 +267,13 @@ def tile_dynamicattentionnetwork_pb_t_kernel(
             if step + TIN_AHEAD + LOAD_AHEAD < GROUPS:
                 load(step + TIN_AHEAD + LOAD_AHEAD)
             if step == 0:
-                nc.gpsimd.dma_start(out=step_bf16[:], in_=step_size.partition_broadcast(P))
-                load_biases(1)
                 spread_biases(0)
                 for branch in ("u", "t"):
                     load_words((1, branch))
                     load_scales((1, branch))
-            if step == 1:
+            if step == TOUT_BEHIND:
                 nc.vector.tensor_copy(out=step_f32[:], in_=step_bf16[:])
+            if step == 6:
                 spread_biases(1)
             if step - TOUT_BEHIND >= 0:
                 transpose_out(step - TOUT_BEHIND)

@@ -27,7 +27,11 @@ GROUPS = BATCH * NODES // ROWS
 GROUPS_PER_BATCH = NODES // ROWS
 INTER_GROUPS = INTER_NODES // ROWS
 
-LOAD_AHEAD = 3
+UNIT_SIZES = (1, 1, 1, 1, 2, 2, 4, 4, 4, 4, 4, 4)
+UNITS = tuple((sum(UNIT_SIZES[:u]), UNIT_SIZES[u]) for u in range(len(UNIT_SIZES)))
+UNIT_OF = {first + g: (u, g) for u, (first, count) in enumerate(UNITS) for g in range(count)}
+GROUP_COLS = ROW_TILES * FEAT
+LOAD_AHEAD = 4
 TIN_AHEAD = 2
 FIRST_SPLIT = 5
 TOUT_BEHIND = 2
@@ -55,9 +59,12 @@ def tile_dynamicattentionnetwork_pb_t_kernel(
     out,
 ):
     nc = tc.nc
-    h_groups = hidden_states.flatten_outer_dims().rearrange("(c p r) k -> c p (r k)", p=P, r=ROW_TILES)
-    a_groups = acc.flatten_outer_dims().rearrange("(c p r) k -> c p (r k)", p=P, r=ROW_TILES)
-    out_groups = out.flatten_outer_dims().rearrange("(c p r) n -> c p (r n)", p=P, r=ROW_TILES)
+
+    def unit_view(tensor, unit):
+        first, count = UNITS[unit]
+        rows = tensor.flatten_outer_dims()[first * ROWS : (first + count) * ROWS, :]
+        return rows.rearrange("(p r) k -> p (r k)", p=P)
+
     given = {
         (0, "t"): (Wt_inter_words, Wt_inter_scales),
         (0, "u"): (Wu_inter_words, Wu_inter_scales),
@@ -68,14 +75,13 @@ def tile_dynamicattentionnetwork_pb_t_kernel(
 
     with ExitStack() as ctx:
         const = ctx.enter_context(tc.tile_pool(name="const", bufs=1))
-        h_pool = ctx.enter_context(tc.tile_pool(name="h_pool", bufs=LOAD_AHEAD + TIN_AHEAD + TOUT_BEHIND + 1))
-        a_pool = ctx.enter_context(tc.tile_pool(name="a_pool", bufs=LOAD_AHEAD + 1))
+        x_pool = ctx.enter_context(tc.tile_pool(name="x_pool", bufs=4))
         grouped_pool = ctx.enter_context(tc.tile_pool(name="grouped_pool", bufs=3))
         split_pool = ctx.enter_context(tc.tile_pool(name="split_pool", bufs=3))
         code_pool = ctx.enter_context(tc.tile_pool(name="code_pool", bufs=3))
         gate_pool = ctx.enter_context(tc.tile_pool(name="gate_pool", bufs=SLICES))
         m_pool = ctx.enter_context(tc.tile_pool(name="m_pool", bufs=TOUT_BEHIND + 1))
-        o_pool = ctx.enter_context(tc.tile_pool(name="o_pool", bufs=GROUPS * ROW_TILES))
+        o_pool = ctx.enter_context(tc.tile_pool(name="o_pool", bufs=48))
         tin_pool = ctx.enter_context(tc.psum_pool(name="tin_pool", bufs=2))
         mm_pool = ctx.enter_context(tc.psum_pool(name="mm_pool", bufs=SLICES))
         tout_pool = ctx.enter_context(tc.psum_pool(name="tout_pool", bufs=2))
@@ -86,12 +92,17 @@ def tile_dynamicattentionnetwork_pb_t_kernel(
         code_tiles = {}
         m_tiles = {}
 
-        def load(group):
-            h_sb = h_pool.tile([P, ROW_TILES * FEAT], BF16, name="h_sb", tag="h_sb")
-            nc.sync.dma_start(out=h_sb[:], in_=h_groups[group])
-            a_sb = a_pool.tile([P, ROW_TILES * FEAT], BF16, name="a_sb", tag="a_sb")
-            nc.sync.dma_start(out=a_sb[:], in_=a_groups[group])
-            x_tiles[group] = (h_sb, a_sb)
+        def load(unit):
+            first, count = UNITS[unit]
+            size = "one" if count == 1 else "many"
+            h_sb = x_pool.tile([P, count * GROUP_COLS], BF16, name="h_sb", tag="h_" + size, bufs=4)
+            nc.sync.dma_start(out=h_sb[:], in_=unit_view(hidden_states, unit))
+            a_bufs = 4 if count == 1 else 3
+            a_sb = x_pool.tile([P, count * GROUP_COLS], BF16, name="a_sb", tag="a_" + size, bufs=a_bufs)
+            nc.sync.dma_start(out=a_sb[:], in_=unit_view(acc, unit))
+            for g in range(count):
+                cols = slice(g * GROUP_COLS, (g + 1) * GROUP_COLS)
+                x_tiles[first + g] = (h_sb[:, cols], a_sb[:, cols])
 
         def load_words(key):
             nc.sync.dma_start(
@@ -110,7 +121,7 @@ def tile_dynamicattentionnetwork_pb_t_kernel(
             a_split = split_pool.tile([P, ROW_TILES, 2, P], F32, name="a_split", tag="a_split")
             nc.scalar.copy(
                 out=a_split[:],
-                in_=x_tiles[group][1][:].bitcast(F32).rearrange("p (i w u) -> p i u w", i=ROW_TILES, u=2),
+                in_=x_tiles[group][1].bitcast(F32).rearrange("p (i w u) -> p i u w", i=ROW_TILES, u=2),
             )
             split_tiles[group] = a_split
 
@@ -119,7 +130,7 @@ def tile_dynamicattentionnetwork_pb_t_kernel(
                 [P, 2, ROWS * PACK], BF16, name="grouped", tag="grouped", align_bytes=64
             )
             for operand in range(2):
-                x_words = x_tiles[group][operand][:].bitcast(F32)
+                x_words = x_tiles[group][operand].bitcast(F32)
                 bank = tin_pool.tile([P, 2, ROWS], F32, name="tin", tag="tin")
                 for i in range(ROW_TILES):
                     for u in range(2):
@@ -184,6 +195,7 @@ def tile_dynamicattentionnetwork_pb_t_kernel(
             m_tiles[group] = m_sb
 
         def transpose_out(group):
+            unit, place = UNIT_OF[group]
             for i in range(ROW_TILES):
                 bank = tout_pool.tile([P, FEAT], F32, name="tout", tag="tout")
                 for j in range(SLICES):
@@ -205,7 +217,8 @@ def tile_dynamicattentionnetwork_pb_t_kernel(
                         op0=MULT,
                         op1=ADD,
                     )
-                    nc.sync.dma_start(out=out_groups[group][:, row_cols], in_=o_sb[:, cols])
+                    out_cols = slice(place * GROUP_COLS + row_cols.start, place * GROUP_COLS + row_cols.stop)
+                    nc.sync.dma_start(out=unit_view(out, unit)[:, out_cols], in_=o_sb[:, cols])
 
         ctx.enter_context(tc.manual_schedule(engines={mybir.EngineType.Pool}))
 
@@ -262,10 +275,12 @@ def tile_dynamicattentionnetwork_pb_t_kernel(
         load_words((0, "t"))
         load_scales((0, "t"))
         load(2)
+        load(3)
 
         for step in range(-TIN_AHEAD, GROUPS + TOUT_BEHIND):
-            if step + TIN_AHEAD + LOAD_AHEAD < GROUPS:
-                load(step + TIN_AHEAD + LOAD_AHEAD)
+            for unit in range(4, len(UNITS)):
+                if UNITS[unit][0] == step + TIN_AHEAD + LOAD_AHEAD:
+                    load(unit)
             if step == 0:
                 spread_biases(0)
                 for branch in ("u", "t"):

from contextlib import ExitStack

import concourse.mybir as mybir
from concourse.masks import make_identity

F32 = mybir.dt.float32
BF16 = mybir.dt.bfloat16
I32 = mybir.dt.int32
U32 = mybir.dt.uint32
U8 = mybir.dt.uint8
FP8X4 = mybir.dt.float8_e4m3fn_x4
ADD = mybir.AluOpType.add
MULT = mybir.AluOpType.mult
TANH = mybir.ActivationFunctionType.Tanh

P = 128
FEAT = 512
PACK = 4
SLICES = FEAT // P
ROW_TILES = 2
ROWS = ROW_TILES * P
WORDS = FEAT // 2
BATCH = 2
NODES = 4096
INTER_NODES = 3072
GROUPS = BATCH * NODES // ROWS
GROUPS_PER_BATCH = NODES // ROWS
INTER_GROUPS = INTER_NODES // ROWS

UNIT_SIZES = (1, 1, 1, 1, 2, 2, 4, 4, 4, 4, 4, 4)
UNITS = tuple((sum(UNIT_SIZES[:u]), UNIT_SIZES[u]) for u in range(len(UNIT_SIZES)))
UNIT_OF = {first + g: (u, g) for u, (first, count) in enumerate(UNITS) for g in range(count)}
GROUP_COLS = ROW_TILES * FEAT
LOAD_AHEAD = 4
TIN_AHEAD = 2
FIRST_SPLIT = 5
TOUT_BEHIND = 2

FLOPS = 2 * 2 * BATCH * NODES * FEAT * FEAT


def tile_dynamicattentionnetwork_pb_t_kernel(
    tc,
    hidden_states,
    acc,
    Wu_inter_words,
    Wu_inter_scales,
    bu_inter,
    Wt_inter_words,
    Wt_inter_scales,
    bt_inter,
    Wu_out_words,
    Wu_out_scales,
    bu_out,
    Wt_out_words,
    Wt_out_scales,
    bt_out,
    step_size,
    out,
):
    nc = tc.nc

    def unit_view(tensor, unit):
        first, count = UNITS[unit]
        rows = tensor.flatten_outer_dims()[first * ROWS : (first + count) * ROWS, :]
        return rows.rearrange("(p r) k -> p (r k)", p=P)

    given = {
        (0, "t"): (Wt_inter_words, Wt_inter_scales),
        (0, "u"): (Wu_inter_words, Wu_inter_scales),
        (1, "t"): (Wt_out_words, Wt_out_scales),
        (1, "u"): (Wu_out_words, Wu_out_scales),
    }
    biases = ((bt_inter, bu_inter), (bt_out, bu_out))

    with ExitStack() as ctx:
        const = ctx.enter_context(tc.tile_pool(name="const", bufs=1))
        x_pool = ctx.enter_context(tc.tile_pool(name="x_pool", bufs=4))
        grouped_pool = ctx.enter_context(tc.tile_pool(name="grouped_pool", bufs=3))
        split_pool = ctx.enter_context(tc.tile_pool(name="split_pool", bufs=3))
        code_pool = ctx.enter_context(tc.tile_pool(name="code_pool", bufs=3))
        gate_pool = ctx.enter_context(tc.tile_pool(name="gate_pool", bufs=SLICES))
        m_pool = ctx.enter_context(tc.tile_pool(name="m_pool", bufs=TOUT_BEHIND + 1))
        o_pool = ctx.enter_context(tc.tile_pool(name="o_pool", bufs=48))
        tin_pool = ctx.enter_context(tc.psum_pool(name="tin_pool", bufs=2))
        mm_pool = ctx.enter_context(tc.psum_pool(name="mm_pool", bufs=SLICES))
        tout_pool = ctx.enter_context(tc.psum_pool(name="tout_pool", bufs=2))

        x_tiles = {}
        split_tiles = {}
        grouped_tiles = {}
        code_tiles = {}
        m_tiles = {}

        def load(unit):
            first, count = UNITS[unit]
            size = "one" if count == 1 else "many"
            h_sb = x_pool.tile([P, count * GROUP_COLS], BF16, name="h_sb", tag="h_" + size, bufs=4)
            nc.sync.dma_start(out=h_sb[:], in_=unit_view(hidden_states, unit))
            a_bufs = 4 if count == 1 else 3
            a_sb = x_pool.tile([P, count * GROUP_COLS], BF16, name="a_sb", tag="a_" + size, bufs=a_bufs)
            nc.sync.dma_start(out=a_sb[:], in_=unit_view(acc, unit))
            for g in range(count):
                cols = slice(g * GROUP_COLS, (g + 1) * GROUP_COLS)
                x_tiles[first + g] = (h_sb[:, cols], a_sb[:, cols])

        def load_words(key):
            nc.sync.dma_start(
                out=w_words[key][:].bitcast(I32),
                in_=given[key][0].rearrange("g p n t -> (g p) (n t)").bitcast(I32),
            )

        def load_scales(key):
            rows = given[key][1].rearrange("g (q r) n -> r (g q) n", r=4)
            for r in range(4):
                nc.sync.dma_start(
                    out=w_planes[key][r:P:32, :].bitcast(I32), in_=rows[r].bitcast(I32)
                )

        def split(group):
            a_split = split_pool.tile([P, ROW_TILES, 2, P], F32, name="a_split", tag="a_split")
            nc.scalar.copy(
                out=a_split[:],
                in_=x_tiles[group][1].bitcast(F32).rearrange("p (i w u) -> p i u w", i=ROW_TILES, u=2),
            )
            split_tiles[group] = a_split

        def transpose_in(group):
            grouped = grouped_pool.tile(
                [P, 2, ROWS * PACK], BF16, name="grouped", tag="grouped", align_bytes=64
            )
            for operand in range(2):
                x_words = x_tiles[group][operand].bitcast(F32)
                bank = tin_pool.tile([P, 2, ROWS], F32, name="tin", tag="tin")
                for i in range(ROW_TILES):
                    for u in range(2):
                        nc.tensor.transpose(
                            out=bank[:, u, i * P : (i + 1) * P],
                            in_=(
                                split_tiles[group][:, i, u, :]
                                if operand == 1 and group >= FIRST_SPLIT
                                else x_words[:, i * WORDS + u : (i + 1) * WORDS : 2]
                            ),
                            identity=ident_f32[:],
                        )
                nc.scalar.copy(
                    out=grouped[:, operand, :].bitcast(F32).rearrange("p (c u) -> p c u", u=2),
                    in_=bank[:].rearrange("p u c -> p c u"),
                )
            grouped_tiles[group] = grouped

        def quantise(group):
            codes = code_pool.tile([P, 2, ROWS], U32, name="codes", tag="codes", align_bytes=64)
            plane = code_pool.tile([P, 2, ROWS], U8, name="plane", tag="plane", align_bytes=64)
            nc.vector.quantize_mx(
                out=codes[:].rearrange("p o c -> p (o c)").bitcast(FP8X4),
                scales=plane[:].rearrange("p o c -> p (o c)"),
                in_=grouped_tiles[group][:].rearrange("p o c -> p (o c)"),
            )
            code_tiles[group] = (codes, plane)

        def multiply(group):
            kind = 0 if group % GROUPS_PER_BATCH < INTER_GROUPS else 1
            codes, plane = code_tiles[group]
            m_sb = m_pool.tile([P, SLICES, ROWS], F32, name="m_sb", tag="m_sb")
            for j in range(SLICES):
                bank = mm_pool.tile([P, 2, ROWS], F32, name="mm", tag="mm")
                for branch, operand in (("u", 1), ("t", 0)):
                    nc.tensor.matmul_mx(
                        out=bank[:, operand, :],
                        lhsT=w_words[(kind, branch)][:, j * P : (j + 1) * P].bitcast(FP8X4),
                        lhsT_scale=w_planes[(kind, branch)][:, j * P : (j + 1) * P],
                        rhs=codes[:, operand, :].bitcast(FP8X4),
                        rhs_scale=plane[:, operand, :],
                        start=True,
                        stop=True,
                    )
                column = SLICES * kind + j
                gate = gate_pool.tile([P, ROWS], F32, name="gate", tag="gate")
                nc.scalar.activation(
                    out=gate[:],
                    in_=bank[:, 0, :],
                    func=TANH,
                    bias=bt_half[:, column : column + 1],
                    scale=0.5,
                )
                nc.vector.scalar_tensor_tensor(
                    out=m_sb[:, j, :],
                    in0=bank[:, 1, :],
                    scalar=bu_cols[:, column : column + 1],
                    in1=gate[:],
                    op0=ADD,
                    op1=MULT,
                )
            m_tiles[group] = m_sb

        def transpose_out(group):
            unit, place = UNIT_OF[group]
            for i in range(ROW_TILES):
                bank = tout_pool.tile([P, FEAT], F32, name="tout", tag="tout")
                for j in range(SLICES):
                    nc.tensor.transpose(
                        out=bank[:, j * P : (j + 1) * P],
                        in_=m_tiles[group][:, j, i * P : (i + 1) * P],
                        identity=ident_f32[:],
                    )
                o_sb = o_pool.tile([P, FEAT], F32, name="o_sb", tag="o_sb")
                pieces = 2 if group == GROUPS - 1 and i == ROW_TILES - 1 else 1
                for piece in range(pieces):
                    cols = slice(piece * FEAT // pieces, (piece + 1) * FEAT // pieces)
                    row_cols = slice(i * FEAT + cols.start, i * FEAT + cols.stop)
                    nc.vector.scalar_tensor_tensor(
                        out=o_sb[:, cols],
                        in0=bank[:, cols],
                        scalar=step_f32[:, 0:1],
                        in1=x_tiles[group][0][:, row_cols],
                        op0=MULT,
                        op1=ADD,
                    )
                    out_cols = slice(place * GROUP_COLS + row_cols.start, place * GROUP_COLS + row_cols.stop)
                    nc.sync.dma_start(out=unit_view(out, unit)[:, out_cols], in_=o_sb[:, cols])

        ctx.enter_context(tc.manual_schedule(engines={mybir.EngineType.Pool}))

        bias_rows = {}
        for kind in range(2):
            bias_rows[kind] = const.tile([P, P], BF16, name="bias_rows", tag="bias_rows%d" % kind)
            nc.vector.memset(bias_rows[kind][:], 0.0)
        w_words = {}
        w_planes = {}
        for key in given:
            w_words[key] = const.tile(
                [P, FEAT], U32, name="w_words", tag="w_words%d%s" % key, align_bytes=64
            )
            w_planes[key] = const.tile(
                [P, FEAT], U8, name="w_plane", tag="w_plane%d%s" % key, align_bytes=64
            )
            nc.vector.memset(w_planes[key][:].bitcast(I32), 0)
        zero = const.tile([P, 1], F32, name="zero")
        nc.vector.memset(zero[:], 0.0)
        table_warm = const.tile([P, 1], F32, name="table_warm")
        nc.scalar.activation(out=table_warm[:], in_=zero[:], func=TANH)

        ident_f32 = const.tile([P, P], F32, name="ident_f32")
        make_identity(nc, ident_f32[:])
        ident_bf16 = const.tile([P, P], BF16, name="ident_bf16")
        nc.vector.tensor_copy(out=ident_bf16[:], in_=ident_f32[:])

        def load_biases(kind):
            for i, bias in enumerate(biases[kind]):
                nc.gpsimd.dma_start(
                    out=bias_rows[kind][SLICES * i : SLICES * (i + 1), :],
                    in_=bias.rearrange("(j p) -> j p", p=P),
                )

        load_biases(0)
        step_bf16 = const.tile([P, 1], BF16, name="step_bf16")
        nc.gpsimd.dma_start(out=step_bf16[:], in_=step_size.partition_broadcast(P))
        load_biases(1)
        bt_half = const.tile([P, 2 * SLICES], F32, name="bt_half")
        bu_cols = const.tile([P, 2 * SLICES], F32, name="bu_cols")
        step_f32 = const.tile([P, 1], F32, name="step_f32")

        def spread_biases(kind):
            bias_ps = tout_pool.tile([P, P], BF16, name="bias_ps", tag="tout")
            nc.tensor.transpose(out=bias_ps[:], in_=bias_rows[kind][:], identity=ident_bf16[:])
            cols = slice(SLICES * kind, SLICES * (kind + 1))
            nc.vector.tensor_scalar_mul(out=bt_half[:, cols], in0=bias_ps[:, 0:SLICES], scalar1=0.5)
            nc.vector.tensor_copy(out=bu_cols[:, cols], in_=bias_ps[:, SLICES : 2 * SLICES])

        load(0)
        load_scales((0, "u"))
        load(1)
        load_words((0, "u"))
        load_words((0, "t"))
        load_scales((0, "t"))
        load(2)
        load(3)

        for step in range(-TIN_AHEAD, GROUPS + TOUT_BEHIND):
            for unit in range(4, len(UNITS)):
                if UNITS[unit][0] == step + TIN_AHEAD + LOAD_AHEAD:
                    load(unit)
            if step == 0:
                spread_biases(0)
                for branch in ("u", "t"):
                    load_words((1, branch))
                    load_scales((1, branch))
            if step == TOUT_BEHIND:
                nc.vector.tensor_copy(out=step_f32[:], in_=step_bf16[:])
            if step == 6:
                spread_biases(1)
            if step - TOUT_BEHIND >= 0:
                transpose_out(step - TOUT_BEHIND)
            if 0 <= step + TIN_AHEAD - 1 < GROUPS:
                quantise(step + TIN_AHEAD - 1)
            if 0 <= step < GROUPS:
                multiply(step)
            if step + TIN_AHEAD < GROUPS:
                transpose_in(step + TIN_AHEAD)
            if FIRST_SPLIT <= step + TIN_AHEAD + 1 < GROUPS:
                split(step + TIN_AHEAD + 1)
